import numpy as np
import ml_dtypes


def mxq(x, axis, fmt="e4m3"):
    dtype, down = {"e4m3": (ml_dtypes.float8_e4m3fn, 7), "e5m2": (ml_dtypes.float8_e5m2, 14)}[fmt]
    v = np.moveaxis(np.asarray(x, np.float32).astype(ml_dtypes.bfloat16).astype(np.float64), axis, -1)
    blocks = v.reshape(v.shape[:-1] + (-1, 32))
    amax = np.abs(blocks).max(-1, keepdims=True)
    byte = np.maximum(np.where(amax > 0, np.frexp(amax)[1] - 1 + 127, 0) - down, 1)
    scale = np.exp2(byte - 127.0)
    codes = (blocks / scale).astype(np.float32).astype(dtype).astype(np.float64)
    return np.moveaxis((codes * scale).reshape(v.shape), -1, axis)


WIDE = False


def mx_kscale(k):
    if not WIDE:
        return np.ones(k)
    levels = np.array([10, -10, 5, -5, 0])
    a = np.random.permutation(np.resize(levels, k // 512 * 4)).reshape(k // 512, 4)
    idx = np.arange(k)
    return np.exp2(a[idx // 512, idx % 128 // 32])


BF16 = ml_dtypes.bfloat16


def bf(x):
    return np.asarray(x, np.float32).astype(BF16)


def f64(x):
    return np.asarray(x).astype(np.float64)


B, N, D, H, K = 8, 1024, 1024, 512, 128
NT = B * N
LN2PI_2 = np.log(2.0 * np.pi) / 2.0


def setup_inputs():
    t = np.exp2(np.round(np.log2(mx_kscale(D)) / 2))
    cent = 0.4 * np.random.standard_normal((B, D))
    idx = np.random.randint(0, B, K)
    return {"xf": bf((np.repeat(cent, N, axis=0) + 0.5 * np.random.standard_normal((NT, D))) * t),
            "mean": bf((0.6 * cent[idx] + 0.1 * np.random.standard_normal((K, D))) * t),
            "var": bf(0.35 * np.exp(0.2 * np.random.standard_normal((K, D))) * t * t)}


def reference(xf, mean, var):
    xv, mv, vv = f64(xf), f64(mean), f64(var)
    inv_var = 1.0 / vv
    quad = ((mxq(xv * xv, 1, "e4m3") @ mxq(inv_var, 1, "e4m3").T)
            - 2.0 * (mxq(xv, 1, "e4m3") @ mxq(mv * inv_var, 1, "e4m3").T)
            + np.sum(mv * mv * inv_var, axis=-1))
    return -0.5 * quad - 0.5 * np.sum(np.log(vv), axis=-1) - xv.shape[-1] * LN2PI_2

@@ -1,0 +1,278 @@
+from contextlib import ExitStack
+import math
+
+import concourse.mybir as mybir
+from concourse.masks import make_identity
+
+F32 = mybir.dt.float32
+BF16 = mybir.dt.bfloat16
+U32 = mybir.dt.uint32
+U8 = mybir.dt.uint8
+FP8X4 = mybir.dt.float8_e4m3fn_x4
+ACT = mybir.ActivationFunctionType
+ALU = mybir.AluOpType
+
+P = 128
+ROWS = 8192
+D = 1024
+COMPS = 128
+FLOPS = 2 * 2 * ROWS * D * COMPS
+
+WORDS = D // 2
+UNITS = ROWS // P
+RU = 2
+ROUNDS = UNITS // RU
+LU = 4
+LOADS = UNITS // LU
+X_BUFS = 8
+G_BUFS = 4
+Q_BUFS = 6
+AHEAD = 3
+
+S_HEAD = (2048, 2048, 0, 384, 512)
+S_STEADY = 912
+S_TAIL = (512, 1280, 1792)
+QW_LATE = 1
+
+
+def s_share(r):
+    if r < len(S_HEAD):
+        return S_HEAD[r]
+    if r >= ROUNDS - len(S_TAIL):
+        return S_TAIL[r - ROUNDS + len(S_TAIL)]
+    return S_STEADY
+
+
+def tile_gaussianmlpbasislayer_pb_t_kernel(tc, xf, mean, var, out):
+    nc = tc.nc
+    with ExitStack() as ctx:
+        ctx.enter_context(tc.manual_schedule())
+        const = ctx.enter_context(tc.tile_pool(name="const", bufs=1))
+        xpool = ctx.enter_context(tc.tile_pool(name="xpool", bufs=X_BUFS))
+        gpool = ctx.enter_context(tc.tile_pool(name="gpool", bufs=G_BUFS))
+        qpool = ctx.enter_context(tc.tile_pool(name="qpool", bufs=Q_BUFS))
+        rpool = ctx.enter_context(tc.tile_pool(name="rpool", bufs=3))
+        psum_t = ctx.enter_context(tc.psum_pool(name="psum_t", bufs=2 * AHEAD))
+        psum_a = ctx.enter_context(tc.psum_pool(name="psum_a", bufs=2))
+
+        ident = const.tile([P, P], F32, name="ident")
+        var_sb = const.tile([P, D], BF16, name="var_sb")
+        mean_sb = const.tile([P, D], BF16, name="mean_sb")
+        iv = const.tile([P, D], F32, name="iv")
+        miv = const.tile([P, D], F32, name="miv")
+        mmiv = const.tile([P, D], F32, name="mmiv")
+        junk = const.tile([P, D], BF16, name="junk")
+        slog = const.tile([P, 1], F32, name="slog")
+        csum = const.tile([P, 1], F32, name="csum")
+        both = const.tile([P, 1], F32, name="both")
+        cfin = const.tile([P, 1], F32, name="cfin")
+        rep = const.tile([P, P], F32, name="rep")
+        const_b = const.tile([P, LU * COMPS], F32, name="const_b")
+        wg = const.tile([P, 4 * 512], BF16, name="wg", align_bytes=64)
+        wq = const.tile([P, 512], U32, name="wq", align_bytes=64)
+        wsc = const.tile([P, 512], U8, name="wsc", align_bytes=64)
+
+        x_tiles = {}
+        banks = {}
+        xg = {}
+        sg = {}
+        codes = {}
+        acc = {}
+
+        def load(l):
+            x_tiles[l] = xpool.tile([P, LU * D], BF16, name="x_sb", tag="x_sb")
+            rows = xf[l * LU * P : (l + 1) * LU * P, :].rearrange("(p t) d -> p t d", t=LU)
+            cuts = 2 if l == 0 else 1
+            step = LU // cuts
+            for c in range(cuts):
+                nc.sync.dma_start(
+                    out=x_tiles[l][:, c * step * D : (c + 1) * step * D].rearrange("p (t d) -> p t d", t=step),
+                    in_=rows[:, c * step : (c + 1) * step, :],
+                )
+
+        def invert(g):
+            half = slice(g * 512, (g + 1) * 512)
+            var_g = var_sb[:, half].rearrange("c (w e) -> c e w", e=2)
+            mean_g = mean_sb[:, half].rearrange("c (w e) -> c e w", e=2)
+            iv_g = iv[:, half].rearrange("c (e w) -> c e w", e=2)
+            miv_g = miv[:, half].rearrange("c (e w) -> c e w", e=2)
+            mmiv_g = mmiv[:, half].rearrange("c (e w) -> c e w", e=2)
+            nc.vector.reciprocal(out=iv_g, in_=var_g)
+            nc.gpsimd.tensor_tensor(out=miv_g, in0=mean_g, in1=iv_g, op=ALU.mult)
+            nc.gpsimd.tensor_tensor(out=mmiv_g, in0=mean_g, in1=miv_g, op=ALU.mult)
+
+        def fill(stage):
+            kind, r = stage
+            pair = []
+            for i in range(2):
+                bank = psum_t.tile([P, WORDS], F32, name="bank", tag="bank")
+                pair.append(bank)
+                if kind == "x":
+                    u = r * RU + i
+                    words = x_tiles[u // LU][:].bitcast(F32)
+                    base = (u % LU) * WORDS
+                    for g in range(2):
+                        for h in range(2):
+                            src = base + (2 * g + h) * P
+                            dst = (2 * h + g) * P
+                            nc.tensor.transpose(bank[:, dst : dst + P], words[:, src : src + P], ident[:])
+                elif kind == "w":
+                    values = (iv, miv)[i]
+                    for h in range(2):
+                        for e in range(2):
+                            src = r * 512 + e * 256 + h * P
+                            dst = (2 * h + e) * P
+                            nc.tensor.transpose(bank[:, dst : dst + P], values[:, src : src + P], ident[:])
+                else:
+                    for t in range(2):
+                        nc.tensor.transpose(bank[:, t * P : (t + 1) * P], rep[:], ident[:])
+            banks[stage] = pair
+
+        def empty_x(r):
+            xg[r] = gpool.tile([P, RU * D], BF16, name="xg", tag="xg", align_bytes=64)
+            sg[r] = gpool.tile([P, RU * D], BF16, name="sg", tag="sg", align_bytes=64)
+            for i in range(RU):
+                bank = banks[("x", r)][i]
+                nc.scalar.copy(
+                    out=xg[r][:].bitcast(F32)[:, i * WORDS : (i + 1) * WORDS].rearrange("p (m h) -> p m h", h=2),
+                    in_=bank[:].rearrange("p (h m) -> p m h", h=2),
+                )
+                first = max(RU * D - s_share(r), i * D)
+                if first < (i + 1) * D:
+                    m0 = (first - i * D) // 4
+                    nc.scalar.activation(
+                        out=sg[r][:, first : (i + 1) * D].rearrange("p (m h e) -> p m h e", h=2, e=2),
+                        in_=bank[:].bitcast(BF16).rearrange("p (h m e) -> p m h e", h=2, e=2)[:, m0:, :, :],
+                        func=ACT.Square,
+                    )
+
+        def square_v(r):
+            n = RU * D - s_share(r)
+            if n > 0:
+                nc.vector.tensor_tensor(out=sg[r][:, :n], in0=xg[r][:, :n], in1=xg[r][:, :n], op=ALU.mult)
+
+        def empty_w(g):
+            for op in range(2):
+                dst = wg[:, (2 * op + g) * 512 : (2 * op + g + 1) * 512].rearrange("p (c t) -> p c t", t=4)
+                src = banks[("w", g)][op][:].rearrange("p (t c) -> p c t", t=4)
+                nc.scalar.activation(out=dst, in_=src, func=ACT.Copy, scale=(-0.5, 1.0)[op])
+
+        def empty_c():
+            for i in range(2):
+                nc.scalar.copy(out=const_b[:, i * 256 : (i + 1) * 256], in_=banks[("c", 0)][i][:, :256])
+
+        def quantise(r):
+            made = []
+            for key, src in (("s", sg[r]), ("x", xg[r])):
+                words = qpool.tile([P, RU * D // 4], U32, name=key + "q", tag=key + "q", align_bytes=64)
+                scales = qpool.tile([P, RU * D // 4], U8, name=key + "c", tag=key + "c", align_bytes=64)
+                made.append((words, scales))
+            for (words, scales), src in zip(reversed(made), (xg[r], sg[r])):
+                nc.vector.quantize_mx(out=words[:].bitcast(FP8X4), scales=scales[:], in_=src[:])
+            codes[r] = made
+
+        def multiply(r):
+            for i in range(RU):
+                j, t = divmod(r * RU + i, LU)
+                if t == 0:
+                    acc[j] = psum_a.tile([P, LU * COMPS], F32, name="acc", tag="acc")
+                n = 0
+                for op in range(2):
+                    words, scales = codes[r][op]
+                    for g in range(2):
+                        a = slice(i * 256 + g * P, i * 256 + (g + 1) * P)
+                        b = slice((2 * op + g) * P, (2 * op + g + 1) * P)
+                        nc.tensor.matmul_mx(
+                            out=acc[j][:, t * COMPS : (t + 1) * COMPS],
+                            lhsT=words[:, a].bitcast(FP8X4),
+                            lhsT_scale=scales[:, a],
+                            rhs=wq[:, b].bitcast(FP8X4),
+                            rhs_scale=wsc[:, b],
+                            start=(n == 0),
+                            stop=(n == 3),
+                        )
+                        n += 1
+
+        def drain(j):
+            res = rpool.tile([P, LU * COMPS], F32, name="res", tag="res")
+            nc.vector.tensor_tensor(out=res[:], in0=acc[j][:], in1=const_b[:], op=ALU.add)
+            rows = out[j * LU * P : (j + 1) * LU * P, :]
+            nc.sync.dma_start(out=rows.rearrange("(p t) k -> p (t k)", t=LU), in_=res[:])
+
+        seq = [("x", 0), ("x", 1), ("w", 0), ("x", 2), ("w", 1), ("x", 3), ("x", 4), ("c", 0)]
+        seq.extend(("x", r) for r in range(5, ROUNDS))
+
+        make_identity(nc, ident[:])
+        nc.scalar.dma_start(out=var_sb[:], in_=var)
+        nc.scalar.dma_start(out=mean_sb[:], in_=mean)
+        for l in range(X_BUFS):
+            load(l)
+        nc.scalar.activation(out=junk[:], in_=var_sb[:], func=ACT.Ln, accum_out=slog[:])
+        for g in range(2):
+            invert(g)
+
+        def fill_and_load(stage):
+            fill(stage)
+            kind, r = stage
+            if kind == "x" and r % 2 == 1 and r // 2 + X_BUFS < LOADS:
+                load(r // 2 + X_BUFS)
+
+        for n in range(AHEAD):
+            fill_and_load(seq[n])
+
+        state = {"weights": False, "const": False, "late": -1}
+        waiting = []
+        full = []
+
+        def multiply_waiting():
+            while waiting:
+                r = waiting.pop(0)
+                multiply(r)
+                if r % 2 == 1:
+                    full.append(r // 2)
+
+        def drain_full(keep):
+            while len(full) > keep:
+                drain(full.pop(0))
+
+        for n, stage in enumerate(seq):
+            kind, r = stage
+            if kind == "x":
+                if r > 0:
+                    quantise(r - 1)
+                    waiting.append(r - 1)
+                ripe = len(full)
+                if state["weights"]:
+                    multiply_waiting()
+                empty_x(r)
+                square_v(r)
+                if state["late"] > 0:
+                    state["late"] -= 1
+                if state["late"] == 0:
+                    state["late"] = -1
+                    nc.vector.quantize_mx(out=wq[:].bitcast(FP8X4), scales=wsc[:], in_=wg[:])
+                    state["weights"] = True
+                if state["const"]:
+                    drain_full(len(full) - ripe)
+            elif kind == "w":
+                if r == 1:
+                    nc.scalar.activation(out=junk[:], in_=mmiv[:], func=ACT.Copy, accum_out=csum[:])
+                    nc.gpsimd.tensor_tensor(out=both[:], in0=csum[:], in1=slog[:], op=ALU.add)
+                    nc.gpsimd.tensor_scalar(
+                        out=cfin[:], in0=both[:], scalar1=-0.5, scalar2=-0.5 * D * math.log(2.0 * math.pi),
+                        op0=ALU.mult, op1=ALU.add,
+                    )
+                empty_w(r)
+                if r == 1:
+                    nc.scalar.activation(out=rep[:], in_=ident[:], func=ACT.Identity, scale=0.0, bias=cfin[:, 0:1])
+                    state["late"] = QW_LATE
+            else:
+                empty_c()
+                state["const"] = True
+                drain_full(0)
+            if n + AHEAD < len(seq):
+                fill_and_load(seq[n + AHEAD])
+        quantise(ROUNDS - 1)
+        waiting.append(ROUNDS - 1)
+        multiply_waiting()
+        drain_full(0)

@@ -8,6 +8,7 @@ F32 = mybir.dt.float32
 BF16 = mybir.dt.bfloat16
 U32 = mybir.dt.uint32
 U8 = mybir.dt.uint8
+I32 = mybir.dt.int32
 FP8X4 = mybir.dt.float8_e4m3fn_x4
 ACT = mybir.ActivationFunctionType
 ALU = mybir.AluOpType
@@ -69,8 +70,8 @@ def tile_gaussianmlpbasislayer_pb_t_kernel(tc, xf, mean, var, out):
         rep = const.tile([P, P], F32, name="rep")
         const_b = const.tile([P, LU * COMPS], F32, name="const_b")
         wg = const.tile([P, 4 * 512], BF16, name="wg", align_bytes=64)
-        wq = const.tile([P, 512], U32, name="wq", align_bytes=64)
-        wsc = const.tile([P, 512], U8, name="wsc", align_bytes=64)
+        wq = const.tile([P, 640], U32, name="wq", align_bytes=64)
+        wsc = const.tile([P, 640], U8, name="wsc", align_bytes=64)
 
         x_tiles = {}
         banks = {}
@@ -181,9 +182,10 @@ def tile_gaussianmlpbasislayer_pb_t_kernel(tc, xf, mean, var, out):
                     words, scales = codes[r][op]
                     for g in range(2):
                         a = slice(i * 256 + g * P, i * 256 + (g + 1) * P)
-                        b = slice((2 * op + g) * P, (2 * op + g + 1) * P)
+                        width = 2 * COMPS if t < LU - 1 else COMPS
+                        b = slice((2 * op + g) * P, (2 * op + g) * P + width)
                         nc.tensor.matmul_mx(
-                            out=acc[j][:, t * COMPS : (t + 1) * COMPS],
+                            out=acc[j][:, t * COMPS : t * COMPS + width],
                             lhsT=words[:, a].bitcast(FP8X4),
                             lhsT_scale=scales[:, a],
                             rhs=wq[:, b].bitcast(FP8X4),
@@ -203,6 +205,8 @@ def tile_gaussianmlpbasislayer_pb_t_kernel(tc, xf, mean, var, out):
         seq.extend(("x", r) for r in range(5, ROUNDS))
 
         make_identity(nc, ident[:])
+        nc.vector.memset(wq[:, 512:].bitcast(I32), 0)
+        nc.vector.memset(wsc[:, 512:].bitcast(I32), 0)
         nc.scalar.dma_start(out=var_sb[:], in_=var)
         nc.scalar.dma_start(out=mean_sb[:], in_=mean)
         for l in range(X_BUFS):
@@ -250,7 +254,7 @@ def tile_gaussianmlpbasislayer_pb_t_kernel(tc, xf, mean, var, out):
                     state["late"] -= 1
                 if state["late"] == 0:
                     state["late"] = -1
-                    nc.vector.quantize_mx(out=wq[:].bitcast(FP8X4), scales=wsc[:], in_=wg[:])
+                    nc.vector.quantize_mx(out=wq[:, :512].bitcast(FP8X4), scales=wsc[:, :512], in_=wg[:])
                     state["weights"] = True
                 if state["const"]:
                     drain_full(len(full) - ripe)

@@ -8,7 +8,6 @@ F32 = mybir.dt.float32
 BF16 = mybir.dt.bfloat16
 U32 = mybir.dt.uint32
 U8 = mybir.dt.uint8
-I32 = mybir.dt.int32
 FP8X4 = mybir.dt.float8_e4m3fn_x4
 ACT = mybir.ActivationFunctionType
 ALU = mybir.AluOpType
@@ -31,7 +30,7 @@ Q_BUFS = 6
 AHEAD = 3
 
 S_HEAD = (2048, 2048, 0, 384, 512)
-S_STEADY = 912
+S_STEADY = 784
 S_TAIL = (512, 1280, 1792)
 QW_LATE = 1
 
@@ -70,8 +69,8 @@ def tile_gaussianmlpbasislayer_pb_t_kernel(tc, xf, mean, var, out):
         rep = const.tile([P, P], F32, name="rep")
         const_b = const.tile([P, LU * COMPS], F32, name="const_b")
         wg = const.tile([P, 4 * 512], BF16, name="wg", align_bytes=64)
-        wq = const.tile([P, 640], U32, name="wq", align_bytes=64)
-        wsc = const.tile([P, 640], U8, name="wsc", align_bytes=64)
+        wq = const.tile([P, 512], U32, name="wq", align_bytes=64)
+        wsc = const.tile([P, 512], U8, name="wsc", align_bytes=64)
 
         x_tiles = {}
         banks = {}
@@ -182,10 +181,9 @@ def tile_gaussianmlpbasislayer_pb_t_kernel(tc, xf, mean, var, out):
                     words, scales = codes[r][op]
                     for g in range(2):
                         a = slice(i * 256 + g * P, i * 256 + (g + 1) * P)
-                        width = 2 * COMPS if t < LU - 1 else COMPS
-                        b = slice((2 * op + g) * P, (2 * op + g) * P + width)
+                        b = slice((2 * op + g) * P, (2 * op + g + 1) * P)
                         nc.tensor.matmul_mx(
-                            out=acc[j][:, t * COMPS : t * COMPS + width],
+                            out=acc[j][:, t * COMPS : (t + 1) * COMPS],
                             lhsT=words[:, a].bitcast(FP8X4),
                             lhsT_scale=scales[:, a],
                             rhs=wq[:, b].bitcast(FP8X4),
@@ -205,8 +203,6 @@ def tile_gaussianmlpbasislayer_pb_t_kernel(tc, xf, mean, var, out):
         seq.extend(("x", r) for r in range(5, ROUNDS))
 
         make_identity(nc, ident[:])
-        nc.vector.memset(wq[:, 512:].bitcast(I32), 0)
-        nc.vector.memset(wsc[:, 512:].bitcast(I32), 0)
         nc.scalar.dma_start(out=var_sb[:], in_=var)
         nc.scalar.dma_start(out=mean_sb[:], in_=mean)
         for l in range(X_BUFS):
@@ -254,7 +250,7 @@ def tile_gaussianmlpbasislayer_pb_t_kernel(tc, xf, mean, var, out):
                     state["late"] -= 1
                 if state["late"] == 0:
                     state["late"] = -1
-                    nc.vector.quantize_mx(out=wq[:, :512].bitcast(FP8X4), scales=wsc[:, :512], in_=wg[:])
+                    nc.vector.quantize_mx(out=wq[:].bitcast(FP8X4), scales=wsc[:], in_=wg[:])
                     state["weights"] = True
                 if state["const"]:
                     drain_full(len(full) - ripe)

@@ -19,28 +19,32 @@ COMPS = 128
 FLOPS = 2 * 2 * ROWS * D * COMPS
 
 WORDS = D // 2
-UNITS = ROWS // P
-RU = 2
-ROUNDS = UNITS // RU
-LU = 4
-LOADS = UNITS // LU
+BU = 4
+BLOCKS = ROWS // (BU * P)
+UNITS = BLOCKS * BU
+T_BANKS = 6
 X_BUFS = 8
-G_BUFS = 4
-Q_BUFS = 6
-AHEAD = 3
+G_BUFS = 3
+Q_BUFS = 4
 
-S_HEAD = (2048, 2048, 0, 384, 512)
-S_STEADY = 784
-S_TAIL = (512, 1280, 1792)
-QW_LATE = 1
+S_SHARE = 1728
+INV_AT = 1
+W_AT = 3
 
 
-def s_share(r):
-    if r < len(S_HEAD):
-        return S_HEAD[r]
-    if r >= ROUNDS - len(S_TAIL):
-        return S_TAIL[r - ROUNDS + len(S_TAIL)]
-    return S_STEADY
+V_UNITS = 2
+S_FIRST = 0
+
+
+S_LAST = 1728
+
+
+def s_share(b):
+    if b == 0:
+        return S_FIRST
+    if b == BLOCKS - 1:
+        return S_LAST
+    return S_SHARE
 
 
 def tile_gaussianmlpbasislayer_pb_t_kernel(tc, xf, mean, var, out):
@@ -52,12 +56,15 @@ def tile_gaussianmlpbasislayer_pb_t_kernel(tc, xf, mean, var, out):
         gpool = ctx.enter_context(tc.tile_pool(name="gpool", bufs=G_BUFS))
         qpool = ctx.enter_context(tc.tile_pool(name="qpool", bufs=Q_BUFS))
         rpool = ctx.enter_context(tc.tile_pool(name="rpool", bufs=3))
-        psum_t = ctx.enter_context(tc.psum_pool(name="psum_t", bufs=2 * AHEAD))
+        psum_t = ctx.enter_context(tc.psum_pool(name="psum_t", bufs=T_BANKS))
         psum_a = ctx.enter_context(tc.psum_pool(name="psum_a", bufs=2))
 
         ident = const.tile([P, P], F32, name="ident")
         var_sb = const.tile([P, D], BF16, name="var_sb")
         mean_sb = const.tile([P, D], BF16, name="mean_sb")
+        lnv = const.tile([P, D], F32, name="lnv")
+        seed = const.tile([P, D], F32, name="seed")
+        prod = const.tile([P, D], F32, name="prod")
         iv = const.tile([P, D], F32, name="iv")
         miv = const.tile([P, D], F32, name="miv")
         mmiv = const.tile([P, D], F32, name="mmiv")
@@ -67,7 +74,7 @@ def tile_gaussianmlpbasislayer_pb_t_kernel(tc, xf, mean, var, out):
         both = const.tile([P, 1], F32, name="both")
         cfin = const.tile([P, 1], F32, name="cfin")
         rep = const.tile([P, P], F32, name="rep")
-        const_b = const.tile([P, LU * COMPS], F32, name="const_b")
+        const_b = const.tile([P, BU * COMPS], F32, name="const_b")
         wg = const.tile([P, 4 * 512], BF16, name="wg", align_bytes=64)
         wq = const.tile([P, 512], U32, name="wq", align_bytes=64)
         wsc = const.tile([P, 512], U8, name="wsc", align_bytes=64)
@@ -79,200 +86,179 @@ def tile_gaussianmlpbasislayer_pb_t_kernel(tc, xf, mean, var, out):
         codes = {}
         acc = {}
 
-        def load(l):
-            x_tiles[l] = xpool.tile([P, LU * D], BF16, name="x_sb", tag="x_sb")
-            rows = xf[l * LU * P : (l + 1) * LU * P, :].rearrange("(p t) d -> p t d", t=LU)
-            cuts = 2 if l == 0 else 1
-            step = LU // cuts
+        def load(b):
+            x_tiles[b] = xpool.tile([P, BU * D], BF16, name="x_sb", tag="x_sb")
+            rows = xf[b * BU * P : (b + 1) * BU * P, :].rearrange("(p t) d -> p t d", t=BU)
+            cuts = 2 if b == 0 else 1
+            step = BU // cuts
             for c in range(cuts):
                 nc.sync.dma_start(
-                    out=x_tiles[l][:, c * step * D : (c + 1) * step * D].rearrange("p (t d) -> p t d", t=step),
+                    out=x_tiles[b][:, c * step * D : (c + 1) * step * D].rearrange("p (t d) -> p t d", t=step),
                     in_=rows[:, c * step : (c + 1) * step, :],
                 )
 
-        def invert(g):
-            half = slice(g * 512, (g + 1) * 512)
-            var_g = var_sb[:, half].rearrange("c (w e) -> c e w", e=2)
-            mean_g = mean_sb[:, half].rearrange("c (w e) -> c e w", e=2)
-            iv_g = iv[:, half].rearrange("c (e w) -> c e w", e=2)
-            miv_g = miv[:, half].rearrange("c (e w) -> c e w", e=2)
-            mmiv_g = mmiv[:, half].rearrange("c (e w) -> c e w", e=2)
-            nc.vector.reciprocal(out=iv_g, in_=var_g)
-            nc.gpsimd.tensor_tensor(out=miv_g, in0=mean_g, in1=iv_g, op=ALU.mult)
-            nc.gpsimd.tensor_tensor(out=mmiv_g, in0=mean_g, in1=miv_g, op=ALU.mult)
+        def transpose_unit(u):
+            if u >= UNITS:
+                return
+            b, t = divmod(u, BU)
+            words = x_tiles[b][:].bitcast(F32)
+            banks[u] = psum_t.tile([P, WORDS], F32, name="bank", tag="bank")
+            for g in range(2):
+                for h in range(2):
+                    src = t * WORDS + (2 * g + h) * P
+                    dst = (2 * h + g) * P
+                    nc.tensor.transpose(banks[u][:, dst : dst + P], words[:, src : src + P], ident[:])
+            if t == BU - 1 and b + X_BUFS < BLOCKS:
+                load(b + X_BUFS)
 
-        def fill(stage):
-            kind, r = stage
-            pair = []
-            for i in range(2):
-                bank = psum_t.tile([P, WORDS], F32, name="bank", tag="bank")
-                pair.append(bank)
-                if kind == "x":
-                    u = r * RU + i
-                    words = x_tiles[u // LU][:].bitcast(F32)
-                    base = (u % LU) * WORDS
-                    for g in range(2):
-                        for h in range(2):
-                            src = base + (2 * g + h) * P
-                            dst = (2 * h + g) * P
-                            nc.tensor.transpose(bank[:, dst : dst + P], words[:, src : src + P], ident[:])
-                elif kind == "w":
-                    values = (iv, miv)[i]
-                    for h in range(2):
-                        for e in range(2):
-                            src = r * 512 + e * 256 + h * P
-                            dst = (2 * h + e) * P
-                            nc.tensor.transpose(bank[:, dst : dst + P], values[:, src : src + P], ident[:])
-                else:
-                    for t in range(2):
-                        nc.tensor.transpose(bank[:, t * P : (t + 1) * P], rep[:], ident[:])
-            banks[stage] = pair
-
-        def empty_x(r):
-            xg[r] = gpool.tile([P, RU * D], BF16, name="xg", tag="xg", align_bytes=64)
-            sg[r] = gpool.tile([P, RU * D], BF16, name="sg", tag="sg", align_bytes=64)
-            for i in range(RU):
-                bank = banks[("x", r)][i]
-                nc.scalar.copy(
-                    out=xg[r][:].bitcast(F32)[:, i * WORDS : (i + 1) * WORDS].rearrange("p (m h) -> p m h", h=2),
-                    in_=bank[:].rearrange("p (h m) -> p m h", h=2),
+        def empty_unit(u):
+            b, t = divmod(u, BU)
+            if t == 0:
+                xg[b] = gpool.tile([P, BU * D], BF16, name="xg", tag="xg", align_bytes=64)
+                sg[b] = gpool.tile([P, BU * D], BF16, name="sg", tag="sg", align_bytes=64)
+            engine_copy = nc.vector.tensor_copy if u < V_UNITS else nc.scalar.copy
+            engine_copy(
+                out=xg[b][:].bitcast(F32)[:, t * WORDS : (t + 1) * WORDS].rearrange("p (m h) -> p m h", h=2),
+                in_=banks[u][:].rearrange("p (h m) -> p m h", h=2),
+            )
+            first = max(BU * D - s_share(b), t * D)
+            if first < (t + 1) * D:
+                nc.scalar.activation(
+                    out=sg[b][:, first : (t + 1) * D].rearrange("p (m h e) -> p m h e", h=2, e=2),
+                    in_=banks[u][:].bitcast(BF16).rearrange("p (h m e) -> p m h e", h=2, e=2)[:, (first - t * D) // 4 :, :, :],
+                    func=ACT.Square,
                 )
-                first = max(RU * D - s_share(r), i * D)
-                if first < (i + 1) * D:
-                    m0 = (first - i * D) // 4
-                    nc.scalar.activation(
-                        out=sg[r][:, first : (i + 1) * D].rearrange("p (m h e) -> p m h e", h=2, e=2),
-                        in_=bank[:].bitcast(BF16).rearrange("p (h m e) -> p m h e", h=2, e=2)[:, m0:, :, :],
-                        func=ACT.Square,
+
+        def square_rest(b):
+            n = BU * D - s_share(b)
+            if n > 0:
+                nc.vector.tensor_tensor(out=sg[b][:, :n], in0=xg[b][:, :n], in1=xg[b][:, :n], op=ALU.mult)
+
+        def quantise(b):
+            codes[b] = []
+            for key in ("s", "x"):
+                words = qpool.tile([P, BU * D // 4], U32, name=key + "q", tag=key + "q", align_bytes=64)
+                scales = qpool.tile([P, BU * D // 4], U8, name=key + "c", tag=key + "c", align_bytes=64)
+                codes[b].append((words, scales))
+            for op, src in ((1, xg[b]), (0, sg[b])):
+                words, scales = codes[b][op]
+                nc.vector.quantize_mx(out=words[:].bitcast(FP8X4), scales=scales[:], in_=src[:])
+
+        def multiply(b, half):
+            if half == 0:
+                acc[b] = psum_a.tile([P, BU * COMPS], F32, name="acc", tag="acc")
+            for t in range(2 * half, 2 * half + 2):
+                for n in range(4):
+                    op, g = divmod(n, 2)
+                    words, scales = codes[b][op]
+                    a = slice(t * 256 + g * P, t * 256 + (g + 1) * P)
+                    w = slice(n * P, (n + 1) * P)
+                    nc.tensor.matmul_mx(
+                        out=acc[b][:, t * COMPS : (t + 1) * COMPS],
+                        lhsT=words[:, a].bitcast(FP8X4),
+                        lhsT_scale=scales[:, a],
+                        rhs=wq[:, w].bitcast(FP8X4),
+                        rhs_scale=wsc[:, w],
+                        start=(n == 0),
+                        stop=(n == 3),
                     )
 
-        def square_v(r):
-            n = RU * D - s_share(r)
-            if n > 0:
-                nc.vector.tensor_tensor(out=sg[r][:, :n], in0=xg[r][:, :n], in1=xg[r][:, :n], op=ALU.mult)
+        def add_and_store(b):
+            res = rpool.tile([P, BU * COMPS], F32, name="res", tag="res")
+            nc.vector.tensor_tensor(out=res[:], in0=acc[b][:], in1=const_b[:], op=ALU.add)
+            rows = out[b * BU * P : (b + 1) * BU * P, :]
+            nc.sync.dma_start(out=rows.rearrange("(p t) k -> p (t k)", t=BU), in_=res[:])
 
-        def empty_w(g):
+        def pairs(tile_ap, g):
+            return tile_ap[:, g * 512 : (g + 1) * 512].rearrange("c (w e) -> c e w", e=2)
+
+        def planes(tile_ap, g):
+            return tile_ap[:, g * 512 : (g + 1) * 512].rearrange("c (e w) -> c e w", e=2)
+
+        def invert(g):
+            half = slice(g * 512, (g + 1) * 512)
+            nc.scalar.activation(out=planes(seed, g), in_=pairs(lnv, g), func=ACT.Exp, scale=-1.0)
+            nc.vector.tensor_tensor(out=planes(prod, g), in0=pairs(var_sb, g), in1=planes(seed, g), op=ALU.mult)
+            nc.vector.scalar_tensor_tensor(
+                out=iv[:, half], in0=prod[:, half], scalar=2.0, in1=seed[:, half], op0=ALU.subtract, op1=ALU.mult
+            )
+            nc.gpsimd.tensor_tensor(out=planes(miv, g), in0=pairs(mean_sb, g), in1=planes(iv, g), op=ALU.mult)
+            nc.gpsimd.tensor_tensor(out=planes(mmiv, g), in0=pairs(mean_sb, g), in1=planes(miv, g), op=ALU.mult)
+
+        w_banks = {}
+
+        def transpose_weights(g):
+            for op, values in enumerate((iv, miv)):
+                w_banks[(g, op)] = psum_a.tile([P, 512], F32, name="acc", tag="acc")
+                for h in range(2):
+                    for e in range(2):
+                        src = g * 512 + e * 256 + h * P
+                        dst = (2 * h + e) * P
+                        nc.tensor.transpose(w_banks[(g, op)][:, dst : dst + P], values[:, src : src + P], ident[:])
+
+        def empty_weights(g):
             for op in range(2):
-                dst = wg[:, (2 * op + g) * 512 : (2 * op + g + 1) * 512].rearrange("p (c t) -> p c t", t=4)
-                src = banks[("w", g)][op][:].rearrange("p (t c) -> p c t", t=4)
-                nc.scalar.activation(out=dst, in_=src, func=ACT.Copy, scale=(-0.5, 1.0)[op])
+                nc.scalar.activation(
+                    out=wg[:, (2 * op + g) * 512 : (2 * op + g + 1) * 512].rearrange("p (c t) -> p c t", t=4),
+                    in_=w_banks[(g, op)][:].rearrange("p (t c) -> p c t", t=4),
+                    func=ACT.Copy,
+                    scale=(0.5, -1.0)[op],
+                )
 
-        def empty_c():
-            for i in range(2):
-                nc.scalar.copy(out=const_b[:, i * 256 : (i + 1) * 256], in_=banks[("c", 0)][i][:, :256])
+        def constant_column():
+            nc.scalar.activation(out=junk[:], in_=mmiv[:], func=ACT.Copy, accum_out=csum[:])
+            nc.gpsimd.tensor_tensor(out=both[:], in0=csum[:], in1=slog[:], op=ALU.subtract)
+            nc.gpsimd.tensor_scalar(
+                out=cfin[:], in0=both[:], scalar1=0.5, scalar2=-0.5 * D * math.log(2.0 * math.pi),
+                op0=ALU.mult, op1=ALU.add,
+            )
 
-        def quantise(r):
-            made = []
-            for key, src in (("s", sg[r]), ("x", xg[r])):
-                words = qpool.tile([P, RU * D // 4], U32, name=key + "q", tag=key + "q", align_bytes=64)
-                scales = qpool.tile([P, RU * D // 4], U8, name=key + "c", tag=key + "c", align_bytes=64)
-                made.append((words, scales))
-            for (words, scales), src in zip(reversed(made), (xg[r], sg[r])):
-                nc.vector.quantize_mx(out=words[:].bitcast(FP8X4), scales=scales[:], in_=src[:])
-            codes[r] = made
+        def constant_rows_start():
+            nc.scalar.activation(out=rep[:], in_=ident[:], func=ACT.Identity, scale=0.0, bias=cfin[:, 0:1])
+            w_banks["c"] = psum_a.tile([P, 512], F32, name="acc", tag="acc")
+            for t in range(BU):
+                nc.tensor.transpose(w_banks["c"][:, t * P : (t + 1) * P], rep[:], ident[:])
 
-        def multiply(r):
-            for i in range(RU):
-                j, t = divmod(r * RU + i, LU)
-                if t == 0:
-                    acc[j] = psum_a.tile([P, LU * COMPS], F32, name="acc", tag="acc")
-                n = 0
-                for op in range(2):
-                    words, scales = codes[r][op]
-                    for g in range(2):
-                        a = slice(i * 256 + g * P, i * 256 + (g + 1) * P)
-                        b = slice((2 * op + g) * P, (2 * op + g + 1) * P)
-                        nc.tensor.matmul_mx(
-                            out=acc[j][:, t * COMPS : (t + 1) * COMPS],
-                            lhsT=words[:, a].bitcast(FP8X4),
-                            lhsT_scale=scales[:, a],
-                            rhs=wq[:, b].bitcast(FP8X4),
-                            rhs_scale=wsc[:, b],
-                            start=(n == 0),
-                            stop=(n == 3),
-                        )
-                        n += 1
+        def constant_rows_end():
+            nc.scalar.copy(out=const_b[:], in_=w_banks["c"][:])
 
-        def drain(j):
-            res = rpool.tile([P, LU * COMPS], F32, name="res", tag="res")
-            nc.vector.tensor_tensor(out=res[:], in0=acc[j][:], in1=const_b[:], op=ALU.add)
-            rows = out[j * LU * P : (j + 1) * LU * P, :]
-            nc.sync.dma_start(out=rows.rearrange("(p t) k -> p (t k)", t=LU), in_=res[:])
+        def block(b, extra=()):
+            if b >= 3:
+                add_and_store(b - 3)
+            if 1 <= b <= BLOCKS:
+                quantise(b - 1)
+            if b == 2:
+                nc.vector.quantize_mx(out=wq[:].bitcast(FP8X4), scales=wsc[:], in_=wg[:])
+            for half in range(2):
+                if 2 <= b <= BLOCKS + 1:
+                    multiply(b - 2, half)
+                if b < BLOCKS:
+                    for t in range(2 * half, 2 * half + 2):
+                        empty_unit(b * BU + t)
+                        transpose_unit(b * BU + t + T_BANKS)
+                        for when, step in extra:
+                            if when == t:
+                                step()
+            if b < BLOCKS:
+                square_rest(b)
 
-        seq = [("x", 0), ("x", 1), ("w", 0), ("x", 2), ("w", 1), ("x", 3), ("x", 4), ("c", 0)]
-        seq.extend(("x", r) for r in range(5, ROUNDS))
+        def weights_out():
+            empty_weights(0)
+            transpose_weights(1)
+            constant_column()
+            empty_weights(1)
+            constant_rows_start()
 
         make_identity(nc, ident[:])
         nc.scalar.dma_start(out=var_sb[:], in_=var)
         nc.scalar.dma_start(out=mean_sb[:], in_=mean)
-        for l in range(X_BUFS):
-            load(l)
-        nc.scalar.activation(out=junk[:], in_=var_sb[:], func=ACT.Ln, accum_out=slog[:])
-        for g in range(2):
-            invert(g)
-
-        def fill_and_load(stage):
-            fill(stage)
-            kind, r = stage
-            if kind == "x" and r % 2 == 1 and r // 2 + X_BUFS < LOADS:
-                load(r // 2 + X_BUFS)
-
-        for n in range(AHEAD):
-            fill_and_load(seq[n])
-
-        state = {"weights": False, "const": False, "late": -1}
-        waiting = []
-        full = []
-
-        def multiply_waiting():
-            while waiting:
-                r = waiting.pop(0)
-                multiply(r)
-                if r % 2 == 1:
-                    full.append(r // 2)
-
-        def drain_full(keep):
-            while len(full) > keep:
-                drain(full.pop(0))
-
-        for n, stage in enumerate(seq):
-            kind, r = stage
-            if kind == "x":
-                if r > 0:
-                    quantise(r - 1)
-                    waiting.append(r - 1)
-                ripe = len(full)
-                if state["weights"]:
-                    multiply_waiting()
-                empty_x(r)
-                square_v(r)
-                if state["late"] > 0:
-                    state["late"] -= 1
-                if state["late"] == 0:
-                    state["late"] = -1
-                    nc.vector.quantize_mx(out=wq[:].bitcast(FP8X4), scales=wsc[:], in_=wg[:])
-                    state["weights"] = True
-                if state["const"]:
-                    drain_full(len(full) - ripe)
-            elif kind == "w":
-                if r == 1:
-                    nc.scalar.activation(out=junk[:], in_=mmiv[:], func=ACT.Copy, accum_out=csum[:])
-                    nc.gpsimd.tensor_tensor(out=both[:], in0=csum[:], in1=slog[:], op=ALU.add)
-                    nc.gpsimd.tensor_scalar(
-                        out=cfin[:], in0=both[:], scalar1=-0.5, scalar2=-0.5 * D * math.log(2.0 * math.pi),
-                        op0=ALU.mult, op1=ALU.add,
-                    )
-                empty_w(r)
-                if r == 1:
-                    nc.scalar.activation(out=rep[:], in_=ident[:], func=ACT.Identity, scale=0.0, bias=cfin[:, 0:1])
-                    state["late"] = QW_LATE
-            else:
-                empty_c()
-                state["const"] = True
-                drain_full(0)
-            if n + AHEAD < len(seq):
-                fill_and_load(seq[n + AHEAD])
-        quantise(ROUNDS - 1)
-        waiting.append(ROUNDS - 1)
-        multiply_waiting()
-        drain_full(0)
+        for b in range(X_BUFS):
+            load(b)
+        nc.scalar.activation(out=lnv[:], in_=var_sb[:], func=ACT.Ln, accum_out=slog[:])
+        for u in range(T_BANKS):
+            transpose_unit(u)
+        block(0, extra=((INV_AT, lambda: (invert(0), invert(1))), (3, lambda: transpose_weights(0)),))
+        block(1, extra=((W_AT, weights_out),))
+        block(2, extra=((0, constant_rows_end),))
+        for b in range(3, BLOCKS + 3):
+            block(b)

@@ -26,25 +26,7 @@ T_BANKS = 6
 X_BUFS = 8
 G_BUFS = 3
 Q_BUFS = 4
-
-S_SHARE = 1728
-INV_AT = 1
-W_AT = 3
-
-
-V_UNITS = 2
-S_FIRST = 0
-
-
-S_LAST = 1728
-
-
-def s_share(b):
-    if b == 0:
-        return S_FIRST
-    if b == BLOCKS - 1:
-        return S_LAST
-    return S_SHARE
+V_COLUMNS = 2176
 
 
 def tile_gaussianmlpbasislayer_pb_t_kernel(tc, xf, mean, var, out):
@@ -62,15 +44,12 @@ def tile_gaussianmlpbasislayer_pb_t_kernel(tc, xf, mean, var, out):
         ident = const.tile([P, P], F32, name="ident")
         var_sb = const.tile([P, D], BF16, name="var_sb")
         mean_sb = const.tile([P, D], BF16, name="mean_sb")
-        lnv = const.tile([P, D], F32, name="lnv")
-        seed = const.tile([P, D], F32, name="seed")
-        prod = const.tile([P, D], F32, name="prod")
         iv = const.tile([P, D], F32, name="iv")
         miv = const.tile([P, D], F32, name="miv")
         mmiv = const.tile([P, D], F32, name="mmiv")
         junk = const.tile([P, D], BF16, name="junk")
         slog = const.tile([P, 1], F32, name="slog")
-        csum = const.tile([P, 1], F32, name="csum")
+        csum = [const.tile([P, 1], F32, name="csum%d" % g) for g in range(2)]
         both = const.tile([P, 1], F32, name="both")
         cfin = const.tile([P, 1], F32, name="cfin")
         rep = const.tile([P, P], F32, name="rep")
@@ -85,11 +64,11 @@ def tile_gaussianmlpbasislayer_pb_t_kernel(tc, xf, mean, var, out):
         sg = {}
         codes = {}
         acc = {}
+        w_banks = {}
 
-        def load(b):
+        def load(b, cuts):
             x_tiles[b] = xpool.tile([P, BU * D], BF16, name="x_sb", tag="x_sb")
             rows = xf[b * BU * P : (b + 1) * BU * P, :].rearrange("(p t) d -> p t d", t=BU)
-            cuts = 2 if b == 0 else 1
             step = BU // cuts
             for c in range(cuts):
                 nc.sync.dma_start(
@@ -98,8 +77,6 @@ def tile_gaussianmlpbasislayer_pb_t_kernel(tc, xf, mean, var, out):
                 )
 
         def transpose_unit(u):
-            if u >= UNITS:
-                return
             b, t = divmod(u, BU)
             words = x_tiles[b][:].bitcast(F32)
             banks[u] = psum_t.tile([P, WORDS], F32, name="bank", tag="bank")
@@ -109,19 +86,18 @@ def tile_gaussianmlpbasislayer_pb_t_kernel(tc, xf, mean, var, out):
                     dst = (2 * h + g) * P
                     nc.tensor.transpose(banks[u][:, dst : dst + P], words[:, src : src + P], ident[:])
             if t == BU - 1 and b + X_BUFS < BLOCKS:
-                load(b + X_BUFS)
+                load(b + X_BUFS, 1)
 
         def empty_unit(u):
             b, t = divmod(u, BU)
             if t == 0:
                 xg[b] = gpool.tile([P, BU * D], BF16, name="xg", tag="xg", align_bytes=64)
                 sg[b] = gpool.tile([P, BU * D], BF16, name="sg", tag="sg", align_bytes=64)
-            engine_copy = nc.vector.tensor_copy if u < V_UNITS else nc.scalar.copy
-            engine_copy(
+            nc.scalar.copy(
                 out=xg[b][:].bitcast(F32)[:, t * WORDS : (t + 1) * WORDS].rearrange("p (m h) -> p m h", h=2),
                 in_=banks[u][:].rearrange("p (h m) -> p m h", h=2),
             )
-            first = max(BU * D - s_share(b), t * D)
+            first = max(V_COLUMNS, t * D)
             if first < (t + 1) * D:
                 nc.scalar.activation(
                     out=sg[b][:, first : (t + 1) * D].rearrange("p (m h e) -> p m h e", h=2, e=2),
@@ -130,9 +106,8 @@ def tile_gaussianmlpbasislayer_pb_t_kernel(tc, xf, mean, var, out):
                 )
 
         def square_rest(b):
-            n = BU * D - s_share(b)
-            if n > 0:
-                nc.vector.tensor_tensor(out=sg[b][:, :n], in0=xg[b][:, :n], in1=xg[b][:, :n], op=ALU.mult)
+            n = V_COLUMNS
+            nc.vector.tensor_tensor(out=sg[b][:, :n], in0=xg[b][:, :n], in1=xg[b][:, :n], op=ALU.mult)
 
         def quantise(b):
             codes[b] = []
@@ -144,24 +119,23 @@ def tile_gaussianmlpbasislayer_pb_t_kernel(tc, xf, mean, var, out):
                 words, scales = codes[b][op]
                 nc.vector.quantize_mx(out=words[:].bitcast(FP8X4), scales=scales[:], in_=src[:])
 
-        def multiply(b, half):
-            if half == 0:
+        def multiply(b, t):
+            if t == 0:
                 acc[b] = psum_a.tile([P, BU * COMPS], F32, name="acc", tag="acc")
-            for t in range(2 * half, 2 * half + 2):
-                for n in range(4):
-                    op, g = divmod(n, 2)
-                    words, scales = codes[b][op]
-                    a = slice(t * 256 + g * P, t * 256 + (g + 1) * P)
-                    w = slice(n * P, (n + 1) * P)
-                    nc.tensor.matmul_mx(
-                        out=acc[b][:, t * COMPS : (t + 1) * COMPS],
-                        lhsT=words[:, a].bitcast(FP8X4),
-                        lhsT_scale=scales[:, a],
-                        rhs=wq[:, w].bitcast(FP8X4),
-                        rhs_scale=wsc[:, w],
-                        start=(n == 0),
-                        stop=(n == 3),
-                    )
+            for n in range(4):
+                op, g = divmod(n, 2)
+                words, scales = codes[b][op]
+                a = slice(t * 256 + g * P, t * 256 + (g + 1) * P)
+                w = slice(n * P, (n + 1) * P)
+                nc.tensor.matmul_mx(
+                    out=acc[b][:, t * COMPS : (t + 1) * COMPS],
+                    lhsT=words[:, a].bitcast(FP8X4),
+                    lhsT_scale=scales[:, a],
+                    rhs=wq[:, w].bitcast(FP8X4),
+                    rhs_scale=wsc[:, w],
+                    start=(n == 0),
+                    stop=(n == 3),
+                )
 
         def add_and_store(b):
             res = rpool.tile([P, BU * COMPS], F32, name="res", tag="res")
@@ -176,16 +150,14 @@ def tile_gaussianmlpbasislayer_pb_t_kernel(tc, xf, mean, var, out):
             return tile_ap[:, g * 512 : (g + 1) * 512].rearrange("c (e w) -> c e w", e=2)
 
         def invert(g):
-            half = slice(g * 512, (g + 1) * 512)
-            nc.scalar.activation(out=planes(seed, g), in_=pairs(lnv, g), func=ACT.Exp, scale=-1.0)
-            nc.vector.tensor_tensor(out=planes(prod, g), in0=pairs(var_sb, g), in1=planes(seed, g), op=ALU.mult)
-            nc.vector.scalar_tensor_tensor(
-                out=iv[:, half], in0=prod[:, half], scalar=2.0, in1=seed[:, half], op0=ALU.subtract, op1=ALU.mult
-            )
-            nc.gpsimd.tensor_tensor(out=planes(miv, g), in0=pairs(mean_sb, g), in1=planes(iv, g), op=ALU.mult)
-            nc.gpsimd.tensor_tensor(out=planes(mmiv, g), in0=pairs(mean_sb, g), in1=planes(miv, g), op=ALU.mult)
+            nc.vector.reciprocal(out=planes(iv, g), in_=pairs(var_sb, g))
 
-        w_banks = {}
+        def times_mean(g):
+            nc.vector.tensor_tensor(out=planes(miv, g), in0=pairs(mean_sb, g), in1=planes(iv, g), op=ALU.mult)
+            nc.vector.scalar_tensor_tensor(
+                out=planes(mmiv, g), in0=pairs(mean_sb, g), scalar=1.0, in1=planes(miv, g),
+                op0=ALU.mult, op1=ALU.mult, accum_out=csum[g][:],
+            )
 
         def transpose_weights(g):
             for op, values in enumerate((iv, miv)):
@@ -202,63 +174,65 @@ def tile_gaussianmlpbasislayer_pb_t_kernel(tc, xf, mean, var, out):
                     out=wg[:, (2 * op + g) * 512 : (2 * op + g + 1) * 512].rearrange("p (c t) -> p c t", t=4),
                     in_=w_banks[(g, op)][:].rearrange("p (t c) -> p c t", t=4),
                     func=ACT.Copy,
-                    scale=(0.5, -1.0)[op],
+                    scale=(-0.5, 1.0)[op],
                 )
 
-        def constant_column():
-            nc.scalar.activation(out=junk[:], in_=mmiv[:], func=ACT.Copy, accum_out=csum[:])
-            nc.gpsimd.tensor_tensor(out=both[:], in0=csum[:], in1=slog[:], op=ALU.subtract)
-            nc.gpsimd.tensor_scalar(
-                out=cfin[:], in0=both[:], scalar1=0.5, scalar2=-0.5 * D * math.log(2.0 * math.pi),
+        def first_weights_out():
+            empty_weights(0)
+            transpose_weights(1)
+
+        def second_weights_out():
+            empty_weights(1)
+            nc.vector.tensor_tensor(out=both[:], in0=csum[0][:], in1=csum[1][:], op=ALU.add)
+            nc.vector.tensor_tensor(out=both[:], in0=both[:], in1=slog[:], op=ALU.add)
+            nc.vector.tensor_scalar(
+                out=cfin[:], in0=both[:], scalar1=-0.5, scalar2=-0.5 * D * math.log(2.0 * math.pi),
                 op0=ALU.mult, op1=ALU.add,
             )
-
-        def constant_rows_start():
             nc.scalar.activation(out=rep[:], in_=ident[:], func=ACT.Identity, scale=0.0, bias=cfin[:, 0:1])
             w_banks["c"] = psum_a.tile([P, 512], F32, name="acc", tag="acc")
             for t in range(BU):
                 nc.tensor.transpose(w_banks["c"][:, t * P : (t + 1) * P], rep[:], ident[:])
 
-        def constant_rows_end():
+        def constant_out():
             nc.scalar.copy(out=const_b[:], in_=w_banks["c"][:])
 
-        def block(b, extra=()):
-            if b >= 3:
-                add_and_store(b - 3)
+        def slot(b, extra=()):
             if 1 <= b <= BLOCKS:
                 quantise(b - 1)
+            if 3 <= b:
+                add_and_store(b - 3)
             if b == 2:
                 nc.vector.quantize_mx(out=wq[:].bitcast(FP8X4), scales=wsc[:], in_=wg[:])
-            for half in range(2):
-                if 2 <= b <= BLOCKS + 1:
-                    multiply(b - 2, half)
+            for t in range(BU):
+                if t % 2 == 0 and 2 <= b <= BLOCKS + 1:
+                    multiply(b - 2, t)
+                    multiply(b - 2, t + 1)
                 if b < BLOCKS:
-                    for t in range(2 * half, 2 * half + 2):
-                        empty_unit(b * BU + t)
+                    empty_unit(b * BU + t)
+                    if b * BU + t + T_BANKS < UNITS:
                         transpose_unit(b * BU + t + T_BANKS)
-                        for when, step in extra:
-                            if when == t:
-                                step()
+                    for when, step in extra:
+                        if when == t:
+                            step()
             if b < BLOCKS:
                 square_rest(b)
 
-        def weights_out():
-            empty_weights(0)
-            transpose_weights(1)
-            constant_column()
-            empty_weights(1)
-            constant_rows_start()
-
         make_identity(nc, ident[:])
         nc.scalar.dma_start(out=var_sb[:], in_=var)
+        load(0, 2)
         nc.scalar.dma_start(out=mean_sb[:], in_=mean)
-        for b in range(X_BUFS):
-            load(b)
-        nc.scalar.activation(out=lnv[:], in_=var_sb[:], func=ACT.Ln, accum_out=slog[:])
+        for b in range(1, X_BUFS):
+            load(b, 1)
+        nc.scalar.activation(out=junk[:], in_=var_sb[:], func=ACT.Ln, accum_out=slog[:])
+        for g in range(2):
+            invert(g)
+        for g in range(2):
+            times_mean(g)
         for u in range(T_BANKS):
             transpose_unit(u)
-        block(0, extra=((INV_AT, lambda: (invert(0), invert(1))), (3, lambda: transpose_weights(0)),))
-        block(1, extra=((W_AT, weights_out),))
-        block(2, extra=((0, constant_rows_end),))
+        slot(0, extra=((1, lambda: transpose_weights(0)),))
+        slot(1, extra=((2, first_weights_out), (3, second_weights_out)))
+        slot(2, extra=((0, constant_out),))
         for b in range(3, BLOCKS + 3):
-            block(b)
+            slot(b)

@@ -26,7 +26,7 @@ T_BANKS = 6
 X_BUFS = 8
 G_BUFS = 3
 Q_BUFS = 4
-V_COLUMNS = 2176
+V_COLUMNS = 2240
 
 
 def tile_gaussianmlpbasislayer_pb_t_kernel(tc, xf, mean, var, out):

@@ -18,15 +18,22 @@ D = 1024
 COMPS = 128
 FLOPS = 2 * 2 * ROWS * D * COMPS
 
-WORDS = D // 2
-BU = 4
-BLOCKS = ROWS // (BU * P)
-UNITS = BLOCKS * BU
-T_BANKS = 6
+PACK = 4
+K_PASS = P * PACK
+PASSES = D // K_PASS
+PAIRS = D // 2
+UNIT_WORDS = D // PACK
+CU = 4
+CHUNKS = ROWS // (CU * P)
+UNITS = CHUNKS * CU
+
+RESULT_BANKS = 2
+UNIT_BANKS = 6
 X_BUFS = 8
-G_BUFS = 3
-Q_BUFS = 4
-V_COLUMNS = 2240
+BF16_BUFS = 3
+CODE_BUFS = 4
+OUT_BUFS = 3
+V_COLUMNS = 2176
 
 
 def tile_gaussianmlpbasislayer_pb_t_kernel(tc, xf, mean, var, out):
@@ -34,147 +41,163 @@ def tile_gaussianmlpbasislayer_pb_t_kernel(tc, xf, mean, var, out):
     with ExitStack() as ctx:
         ctx.enter_context(tc.manual_schedule())
         const = ctx.enter_context(tc.tile_pool(name="const", bufs=1))
-        xpool = ctx.enter_context(tc.tile_pool(name="xpool", bufs=X_BUFS))
-        gpool = ctx.enter_context(tc.tile_pool(name="gpool", bufs=G_BUFS))
-        qpool = ctx.enter_context(tc.tile_pool(name="qpool", bufs=Q_BUFS))
-        rpool = ctx.enter_context(tc.tile_pool(name="rpool", bufs=3))
-        psum_t = ctx.enter_context(tc.psum_pool(name="psum_t", bufs=T_BANKS))
-        psum_a = ctx.enter_context(tc.psum_pool(name="psum_a", bufs=2))
+        x_pool = ctx.enter_context(tc.tile_pool(name="x_pool", bufs=X_BUFS))
+        bf16_pool = ctx.enter_context(tc.tile_pool(name="bf16_pool", bufs=BF16_BUFS))
+        code_pool = ctx.enter_context(tc.tile_pool(name="code_pool", bufs=CODE_BUFS))
+        out_pool = ctx.enter_context(tc.tile_pool(name="out_pool", bufs=OUT_BUFS))
+        unit_psum = ctx.enter_context(tc.psum_pool(name="unit_psum", bufs=UNIT_BANKS))
+        result_psum = ctx.enter_context(tc.psum_pool(name="result_psum", bufs=RESULT_BANKS))
 
         ident = const.tile([P, P], F32, name="ident")
         var_sb = const.tile([P, D], BF16, name="var_sb")
         mean_sb = const.tile([P, D], BF16, name="mean_sb")
-        iv = const.tile([P, D], F32, name="iv")
-        miv = const.tile([P, D], F32, name="miv")
-        mmiv = const.tile([P, D], F32, name="mmiv")
-        junk = const.tile([P, D], BF16, name="junk")
-        slog = const.tile([P, 1], F32, name="slog")
-        csum = [const.tile([P, 1], F32, name="csum%d" % g) for g in range(2)]
-        both = const.tile([P, 1], F32, name="both")
-        cfin = const.tile([P, 1], F32, name="cfin")
-        rep = const.tile([P, P], F32, name="rep")
-        const_b = const.tile([P, BU * COMPS], F32, name="const_b")
-        wg = const.tile([P, 4 * 512], BF16, name="wg", align_bytes=64)
-        wq = const.tile([P, 512], U32, name="wq", align_bytes=64)
-        wsc = const.tile([P, 512], U8, name="wsc", align_bytes=64)
+        inv_var = const.tile([P, D], F32, name="inv_var")
+        mean_inv_var = const.tile([P, D], F32, name="mean_inv_var")
+        mean2_inv_var = const.tile([P, D], F32, name="mean2_inv_var")
+        logs = const.tile([P, D], BF16, name="logs")
+        log_sum = const.tile([P, 1], F32, name="log_sum")
+        c_part = [const.tile([P, 1], F32, name="c_part%d" % g) for g in range(PASSES)]
+        sums = const.tile([P, 1], F32, name="sums")
+        constant = const.tile([P, 1], F32, name="constant")
+        constant_wide = const.tile([P, P], F32, name="constant_wide")
+        constant_rows = const.tile([P, CU * COMPS], F32, name="constant_rows")
+        w_bf16 = const.tile([P, 2 * PASSES * K_PASS], BF16, name="w_bf16", align_bytes=64)
+        w_words = const.tile([P, 2 * PASSES * COMPS], U32, name="w_words", align_bytes=64)
+        w_scales = const.tile([P, 2 * PASSES * COMPS], U8, name="w_scales", align_bytes=64)
 
         x_tiles = {}
-        banks = {}
-        xg = {}
-        sg = {}
+        unit_banks = {}
+        x_bf16 = {}
+        sq_bf16 = {}
         codes = {}
-        acc = {}
+        results = {}
         w_banks = {}
 
-        def load(b, cuts):
-            x_tiles[b] = xpool.tile([P, BU * D], BF16, name="x_sb", tag="x_sb")
-            rows = xf[b * BU * P : (b + 1) * BU * P, :].rearrange("(p t) d -> p t d", t=BU)
-            step = BU // cuts
-            for c in range(cuts):
+        def load(c, cuts):
+            x_tiles[c] = x_pool.tile([P, CU * D], BF16, name="x_sb", tag="x_sb")
+            rows = xf[c * CU * P : (c + 1) * CU * P, :].rearrange("(p t) d -> p t d", t=CU)
+            step = CU // cuts
+            for i in range(cuts):
                 nc.sync.dma_start(
-                    out=x_tiles[b][:, c * step * D : (c + 1) * step * D].rearrange("p (t d) -> p t d", t=step),
-                    in_=rows[:, c * step : (c + 1) * step, :],
+                    out=x_tiles[c][:, i * step * D : (i + 1) * step * D].rearrange("p (t d) -> p t d", t=step),
+                    in_=rows[:, i * step : (i + 1) * step, :],
                 )
 
         def transpose_unit(u):
-            b, t = divmod(u, BU)
-            words = x_tiles[b][:].bitcast(F32)
-            banks[u] = psum_t.tile([P, WORDS], F32, name="bank", tag="bank")
-            for g in range(2):
+            c, t = divmod(u, CU)
+            as_pairs = x_tiles[c][:].bitcast(F32)
+            unit_banks[u] = unit_psum.tile([P, PAIRS], F32, name="unit_bank", tag="unit_bank")
+            for g in range(PASSES):
                 for h in range(2):
-                    src = t * WORDS + (2 * g + h) * P
+                    src = t * PAIRS + (2 * g + h) * P
                     dst = (2 * h + g) * P
-                    nc.tensor.transpose(banks[u][:, dst : dst + P], words[:, src : src + P], ident[:])
-            if t == BU - 1 and b + X_BUFS < BLOCKS:
-                load(b + X_BUFS, 1)
+                    nc.tensor.transpose(unit_banks[u][:, dst : dst + P], as_pairs[:, src : src + P], ident[:])
+            if t == CU - 1 and c + X_BUFS < CHUNKS:
+                load(c + X_BUFS, 1)
 
         def empty_unit(u):
-            b, t = divmod(u, BU)
+            c, t = divmod(u, CU)
             if t == 0:
-                xg[b] = gpool.tile([P, BU * D], BF16, name="xg", tag="xg", align_bytes=64)
-                sg[b] = gpool.tile([P, BU * D], BF16, name="sg", tag="sg", align_bytes=64)
+                x_bf16[c] = bf16_pool.tile([P, CU * D], BF16, name="x_bf16", tag="x_bf16", align_bytes=64)
+                sq_bf16[c] = bf16_pool.tile([P, CU * D], BF16, name="sq_bf16", tag="sq_bf16", align_bytes=64)
             nc.scalar.copy(
-                out=xg[b][:].bitcast(F32)[:, t * WORDS : (t + 1) * WORDS].rearrange("p (m h) -> p m h", h=2),
-                in_=banks[u][:].rearrange("p (h m) -> p m h", h=2),
+                out=x_bf16[c][:].bitcast(F32)[:, t * PAIRS : (t + 1) * PAIRS].rearrange("p (m h) -> p m h", h=2),
+                in_=unit_banks[u][:].rearrange("p (h m) -> p m h", h=2),
             )
             first = max(V_COLUMNS, t * D)
             if first < (t + 1) * D:
+                as_bf16 = unit_banks[u][:].bitcast(BF16).rearrange("p (h m e) -> p m h e", h=2, e=2)
                 nc.scalar.activation(
-                    out=sg[b][:, first : (t + 1) * D].rearrange("p (m h e) -> p m h e", h=2, e=2),
-                    in_=banks[u][:].bitcast(BF16).rearrange("p (h m e) -> p m h e", h=2, e=2)[:, (first - t * D) // 4 :, :, :],
+                    out=sq_bf16[c][:, first : (t + 1) * D].rearrange("p (m h e) -> p m h e", h=2, e=2),
+                    in_=as_bf16[:, (first - t * D) // PACK :, :, :],
                     func=ACT.Square,
                 )
 
-        def square_rest(b):
+        def square_rest(c):
             n = V_COLUMNS
-            nc.vector.tensor_tensor(out=sg[b][:, :n], in0=xg[b][:, :n], in1=xg[b][:, :n], op=ALU.mult)
+            nc.vector.tensor_tensor(out=sq_bf16[c][:, :n], in0=x_bf16[c][:, :n], in1=x_bf16[c][:, :n], op=ALU.mult)
 
-        def quantise(b):
-            codes[b] = []
-            for key in ("s", "x"):
-                words = qpool.tile([P, BU * D // 4], U32, name=key + "q", tag=key + "q", align_bytes=64)
-                scales = qpool.tile([P, BU * D // 4], U8, name=key + "c", tag=key + "c", align_bytes=64)
-                codes[b].append((words, scales))
-            for op, src in ((1, xg[b]), (0, sg[b])):
-                words, scales = codes[b][op]
-                nc.vector.quantize_mx(out=words[:].bitcast(FP8X4), scales=scales[:], in_=src[:])
+        def quantise(c):
+            codes[c] = []
+            for key in ("sq", "x"):
+                words = code_pool.tile(
+                    [P, CU * UNIT_WORDS], U32, name=key + "_words", tag=key + "_words", align_bytes=64
+                )
+                scales = code_pool.tile(
+                    [P, CU * UNIT_WORDS], U8, name=key + "_scales", tag=key + "_scales", align_bytes=64
+                )
+                codes[c].append((words, scales))
+            for operand, values in ((1, x_bf16[c]), (0, sq_bf16[c])):
+                words, scales = codes[c][operand]
+                nc.vector.quantize_mx(out=words[:].bitcast(FP8X4), scales=scales[:], in_=values[:])
 
-        def multiply(b, t):
+        def multiply(c, t):
             if t == 0:
-                acc[b] = psum_a.tile([P, BU * COMPS], F32, name="acc", tag="acc")
-            for n in range(4):
-                op, g = divmod(n, 2)
-                words, scales = codes[b][op]
-                a = slice(t * 256 + g * P, t * 256 + (g + 1) * P)
-                w = slice(n * P, (n + 1) * P)
+                results[c] = result_psum.tile([P, CU * COMPS], F32, name="result_bank", tag="result_bank")
+            last = 2 * PASSES - 1
+            for n in range(last + 1):
+                operand, g = divmod(n, PASSES)
+                words, scales = codes[c][operand]
+                unit_cols = slice(t * UNIT_WORDS + g * P, t * UNIT_WORDS + (g + 1) * P)
+                w_cols = slice(n * COMPS, (n + 1) * COMPS)
                 nc.tensor.matmul_mx(
-                    out=acc[b][:, t * COMPS : (t + 1) * COMPS],
-                    lhsT=words[:, a].bitcast(FP8X4),
-                    lhsT_scale=scales[:, a],
-                    rhs=wq[:, w].bitcast(FP8X4),
-                    rhs_scale=wsc[:, w],
+                    out=results[c][:, t * COMPS : (t + 1) * COMPS],
+                    lhsT=words[:, unit_cols].bitcast(FP8X4),
+                    lhsT_scale=scales[:, unit_cols],
+                    rhs=w_words[:, w_cols].bitcast(FP8X4),
+                    rhs_scale=w_scales[:, w_cols],
                     start=(n == 0),
-                    stop=(n == 3),
+                    stop=(n == last),
                 )
 
-        def add_and_store(b):
-            res = rpool.tile([P, BU * COMPS], F32, name="res", tag="res")
-            nc.vector.tensor_tensor(out=res[:], in0=acc[b][:], in1=const_b[:], op=ALU.add)
-            rows = out[b * BU * P : (b + 1) * BU * P, :]
-            nc.sync.dma_start(out=rows.rearrange("(p t) k -> p (t k)", t=BU), in_=res[:])
+        def add_and_store(c):
+            finished = out_pool.tile([P, CU * COMPS], F32, name="finished", tag="finished")
+            nc.vector.tensor_tensor(out=finished[:], in0=results[c][:], in1=constant_rows[:], op=ALU.add)
+            rows = out[c * CU * P : (c + 1) * CU * P, :]
+            nc.sync.dma_start(out=rows.rearrange("(p t) k -> p (t k)", t=CU), in_=finished[:])
 
-        def pairs(tile_ap, g):
-            return tile_ap[:, g * 512 : (g + 1) * 512].rearrange("c (w e) -> c e w", e=2)
 
-        def planes(tile_ap, g):
-            return tile_ap[:, g * 512 : (g + 1) * 512].rearrange("c (e w) -> c e w", e=2)
+        def as_in_dram(tile_ap, g):
+            return tile_ap[:, g * K_PASS : (g + 1) * K_PASS].rearrange("k (w e) -> k e w", e=2)
+
+        def in_planes(tile_ap, g):
+            return tile_ap[:, g * K_PASS : (g + 1) * K_PASS].rearrange("k (e w) -> k e w", e=2)
 
         def invert(g):
-            nc.vector.reciprocal(out=planes(iv, g), in_=pairs(var_sb, g))
+            nc.vector.reciprocal(out=in_planes(inv_var, g), in_=as_in_dram(var_sb, g))
 
         def times_mean(g):
-            nc.vector.tensor_tensor(out=planes(miv, g), in0=pairs(mean_sb, g), in1=planes(iv, g), op=ALU.mult)
+            nc.vector.tensor_tensor(
+                out=in_planes(mean_inv_var, g), in0=as_in_dram(mean_sb, g), in1=in_planes(inv_var, g), op=ALU.mult
+            )
             nc.vector.scalar_tensor_tensor(
-                out=planes(mmiv, g), in0=pairs(mean_sb, g), scalar=1.0, in1=planes(miv, g),
-                op0=ALU.mult, op1=ALU.mult, accum_out=csum[g][:],
+                out=in_planes(mean2_inv_var, g),
+                in0=as_in_dram(mean_sb, g),
+                scalar=1.0,
+                in1=in_planes(mean_inv_var, g),
+                op0=ALU.mult,
+                op1=ALU.mult,
+                accum_out=c_part[g][:],
             )
 
         def transpose_weights(g):
-            for op, values in enumerate((iv, miv)):
-                w_banks[(g, op)] = psum_a.tile([P, 512], F32, name="acc", tag="acc")
+            for operand, values in enumerate((inv_var, mean_inv_var)):
+                bank = result_psum.tile([P, PACK * COMPS], F32, name="result_bank", tag="result_bank")
                 for h in range(2):
                     for e in range(2):
-                        src = g * 512 + e * 256 + h * P
+                        src = g * K_PASS + e * (K_PASS // 2) + h * P
                         dst = (2 * h + e) * P
-                        nc.tensor.transpose(w_banks[(g, op)][:, dst : dst + P], values[:, src : src + P], ident[:])
+                        nc.tensor.transpose(bank[:, dst : dst + P], values[:, src : src + P], ident[:])
+                w_banks[(g, operand)] = bank
 
         def empty_weights(g):
-            for op in range(2):
+            for operand in range(2):
+                n = PASSES * operand + g
                 nc.scalar.activation(
-                    out=wg[:, (2 * op + g) * 512 : (2 * op + g + 1) * 512].rearrange("p (c t) -> p c t", t=4),
-                    in_=w_banks[(g, op)][:].rearrange("p (t c) -> p c t", t=4),
+                    out=w_bf16[:, n * K_PASS : (n + 1) * K_PASS].rearrange("p (k t) -> p k t", t=PACK),
+                    in_=w_banks[(g, operand)][:].rearrange("p (t k) -> p k t", t=PACK),
                     func=ACT.Copy,
-                    scale=(-0.5, 1.0)[op],
+                    scale=(-0.5, 1.0)[operand],
                 )
 
         def first_weights_out():
@@ -183,56 +206,62 @@ def tile_gaussianmlpbasislayer_pb_t_kernel(tc, xf, mean, var, out):
 
         def second_weights_out():
             empty_weights(1)
-            nc.vector.tensor_tensor(out=both[:], in0=csum[0][:], in1=csum[1][:], op=ALU.add)
-            nc.vector.tensor_tensor(out=both[:], in0=both[:], in1=slog[:], op=ALU.add)
+            nc.vector.tensor_tensor(out=sums[:], in0=c_part[0][:], in1=c_part[1][:], op=ALU.add)
+            nc.vector.tensor_tensor(out=sums[:], in0=sums[:], in1=log_sum[:], op=ALU.add)
             nc.vector.tensor_scalar(
-                out=cfin[:], in0=both[:], scalar1=-0.5, scalar2=-0.5 * D * math.log(2.0 * math.pi),
-                op0=ALU.mult, op1=ALU.add,
+                out=constant[:],
+                in0=sums[:],
+                scalar1=-0.5,
+                scalar2=-0.5 * D * math.log(2.0 * math.pi),
+                op0=ALU.mult,
+                op1=ALU.add,
             )
-            nc.scalar.activation(out=rep[:], in_=ident[:], func=ACT.Identity, scale=0.0, bias=cfin[:, 0:1])
-            w_banks["c"] = psum_a.tile([P, 512], F32, name="acc", tag="acc")
-            for t in range(BU):
-                nc.tensor.transpose(w_banks["c"][:, t * P : (t + 1) * P], rep[:], ident[:])
+            nc.scalar.activation(
+                out=constant_wide[:], in_=ident[:], func=ACT.Identity, scale=0.0, bias=constant[:, 0:1]
+            )
+            w_banks["constant"] = result_psum.tile([P, CU * COMPS], F32, name="result_bank", tag="result_bank")
+            for t in range(CU):
+                nc.tensor.transpose(w_banks["constant"][:, t * P : (t + 1) * P], constant_wide[:], ident[:])
 
         def constant_out():
-            nc.scalar.copy(out=const_b[:], in_=w_banks["c"][:])
+            nc.scalar.copy(out=constant_rows[:], in_=w_banks["constant"][:])
 
-        def slot(b, extra=()):
-            if 1 <= b <= BLOCKS:
-                quantise(b - 1)
-            if 3 <= b:
-                add_and_store(b - 3)
-            if b == 2:
-                nc.vector.quantize_mx(out=wq[:].bitcast(FP8X4), scales=wsc[:], in_=wg[:])
-            for t in range(BU):
-                if t % 2 == 0 and 2 <= b <= BLOCKS + 1:
-                    multiply(b - 2, t)
-                    multiply(b - 2, t + 1)
-                if b < BLOCKS:
-                    empty_unit(b * BU + t)
-                    if b * BU + t + T_BANKS < UNITS:
-                        transpose_unit(b * BU + t + T_BANKS)
+        def slot(s, extra=()):
+            if 1 <= s <= CHUNKS:
+                quantise(s - 1)
+            if 3 <= s:
+                add_and_store(s - 3)
+            if s == 2:
+                nc.vector.quantize_mx(out=w_words[:].bitcast(FP8X4), scales=w_scales[:], in_=w_bf16[:])
+            for t in range(CU):
+                if t % 2 == 0 and 2 <= s <= CHUNKS + 1:
+                    multiply(s - 2, t)
+                    multiply(s - 2, t + 1)
+                if s < CHUNKS:
+                    empty_unit(s * CU + t)
+                    if s * CU + t + UNIT_BANKS < UNITS:
+                        transpose_unit(s * CU + t + UNIT_BANKS)
                     for when, step in extra:
                         if when == t:
                             step()
-            if b < BLOCKS:
-                square_rest(b)
+            if s < CHUNKS:
+                square_rest(s)
 
         make_identity(nc, ident[:])
         nc.scalar.dma_start(out=var_sb[:], in_=var)
         load(0, 2)
         nc.scalar.dma_start(out=mean_sb[:], in_=mean)
-        for b in range(1, X_BUFS):
-            load(b, 1)
-        nc.scalar.activation(out=junk[:], in_=var_sb[:], func=ACT.Ln, accum_out=slog[:])
-        for g in range(2):
+        for c in range(1, X_BUFS):
+            load(c, 1)
+        nc.scalar.activation(out=logs[:], in_=var_sb[:], func=ACT.Ln, accum_out=log_sum[:])
+        for g in range(PASSES):
             invert(g)
-        for g in range(2):
+        for g in range(PASSES):
             times_mean(g)
-        for u in range(T_BANKS):
+        for u in range(UNIT_BANKS):
             transpose_unit(u)
         slot(0, extra=((1, lambda: transpose_weights(0)),))
         slot(1, extra=((2, first_weights_out), (3, second_weights_out)))
         slot(2, extra=((0, constant_out),))
-        for b in range(3, BLOCKS + 3):
-            slot(b)
+        for s in range(3, CHUNKS + 3):
+            slot(s)

from contextlib import ExitStack
import math

import concourse.mybir as mybir
from concourse.masks import make_identity

F32 = mybir.dt.float32
BF16 = mybir.dt.bfloat16
U32 = mybir.dt.uint32
U8 = mybir.dt.uint8
FP8X4 = mybir.dt.float8_e4m3fn_x4
ACT = mybir.ActivationFunctionType
ALU = mybir.AluOpType

P = 128
ROWS = 8192
D = 1024
COMPS = 128
FLOPS = 2 * 2 * ROWS * D * COMPS

PACK = 4
K_PASS = P * PACK
PASSES = D // K_PASS
PAIRS = D // 2
UNIT_WORDS = D // PACK
CU = 4
CHUNKS = ROWS // (CU * P)
UNITS = CHUNKS * CU

RESULT_BANKS = 2
UNIT_BANKS = 6
X_BUFS = 8
BF16_BUFS = 3
CODE_BUFS = 4
OUT_BUFS = 3
V_COLUMNS = 2176


def tile_gaussianmlpbasislayer_pb_t_kernel(tc, xf, mean, var, out):
    nc = tc.nc
    with ExitStack() as ctx:
        ctx.enter_context(tc.manual_schedule())
        const = ctx.enter_context(tc.tile_pool(name="const", bufs=1))
        x_pool = ctx.enter_context(tc.tile_pool(name="x_pool", bufs=X_BUFS))
        bf16_pool = ctx.enter_context(tc.tile_pool(name="bf16_pool", bufs=BF16_BUFS))
        code_pool = ctx.enter_context(tc.tile_pool(name="code_pool", bufs=CODE_BUFS))
        out_pool = ctx.enter_context(tc.tile_pool(name="out_pool", bufs=OUT_BUFS))
        unit_psum = ctx.enter_context(tc.psum_pool(name="unit_psum", bufs=UNIT_BANKS))
        result_psum = ctx.enter_context(tc.psum_pool(name="result_psum", bufs=RESULT_BANKS))

        ident = const.tile([P, P], F32, name="ident")
        var_sb = const.tile([P, D], BF16, name="var_sb")
        mean_sb = const.tile([P, D], BF16, name="mean_sb")
        inv_var = const.tile([P, D], F32, name="inv_var")
        mean_inv_var = const.tile([P, D], F32, name="mean_inv_var")
        mean2_inv_var = const.tile([P, D], F32, name="mean2_inv_var")
        logs = const.tile([P, D], BF16, name="logs")
        log_sum = const.tile([P, 1], F32, name="log_sum")
        c_part = [const.tile([P, 1], F32, name="c_part%d" % g) for g in range(PASSES)]
        sums = const.tile([P, 1], F32, name="sums")
        constant = const.tile([P, 1], F32, name="constant")
        constant_wide = const.tile([P, P], F32, name="constant_wide")
        constant_rows = const.tile([P, CU * COMPS], F32, name="constant_rows")
        w_bf16 = const.tile([P, 2 * PASSES * K_PASS], BF16, name="w_bf16", align_bytes=64)
        w_words = const.tile([P, 2 * PASSES * COMPS], U32, name="w_words", align_bytes=64)
        w_scales = const.tile([P, 2 * PASSES * COMPS], U8, name="w_scales", align_bytes=64)

        x_tiles = {}
        unit_banks = {}
        x_bf16 = {}
        sq_bf16 = {}
        codes = {}
        results = {}
        w_banks = {}

        def load(c, cuts):
            x_tiles[c] = x_pool.tile([P, CU * D], BF16, name="x_sb", tag="x_sb")
            rows = xf[c * CU * P : (c + 1) * CU * P, :].rearrange("(p t) d -> p t d", t=CU)
            step = CU // cuts
            for i in range(cuts):
                nc.sync.dma_start(
                    out=x_tiles[c][:, i * step * D : (i + 1) * step * D].rearrange("p (t d) -> p t d", t=step),
                    in_=rows[:, i * step : (i + 1) * step, :],
                )

        def transpose_unit(u):
            c, t = divmod(u, CU)
            as_pairs = x_tiles[c][:].bitcast(F32)
            unit_banks[u] = unit_psum.tile([P, PAIRS], F32, name="unit_bank", tag="unit_bank")
            for g in range(PASSES):
                for h in range(2):
                    src = t * PAIRS + (2 * g + h) * P
                    dst = (2 * h + g) * P
                    nc.tensor.transpose(unit_banks[u][:, dst : dst + P], as_pairs[:, src : src + P], ident[:])
            if t == CU - 1 and c + X_BUFS < CHUNKS:
                load(c + X_BUFS, 1)

        def empty_unit(u):
            c, t = divmod(u, CU)
            if t == 0:
                x_bf16[c] = bf16_pool.tile([P, CU * D], BF16, name="x_bf16", tag="x_bf16", align_bytes=64)
                sq_bf16[c] = bf16_pool.tile([P, CU * D], BF16, name="sq_bf16", tag="sq_bf16", align_bytes=64)
            nc.scalar.copy(
                out=x_bf16[c][:].bitcast(F32)[:, t * PAIRS : (t + 1) * PAIRS].rearrange("p (m h) -> p m h", h=2),
                in_=unit_banks[u][:].rearrange("p (h m) -> p m h", h=2),
            )
            first = max(V_COLUMNS, t * D)
            if first < (t + 1) * D:
                as_bf16 = unit_banks[u][:].bitcast(BF16).rearrange("p (h m e) -> p m h e", h=2, e=2)
                nc.scalar.activation(
                    out=sq_bf16[c][:, first : (t + 1) * D].rearrange("p (m h e) -> p m h e", h=2, e=2),
                    in_=as_bf16[:, (first - t * D) // PACK :, :, :],
                    func=ACT.Square,
                )

        def square_rest(c):
            n = V_COLUMNS
            nc.vector.tensor_tensor(out=sq_bf16[c][:, :n], in0=x_bf16[c][:, :n], in1=x_bf16[c][:, :n], op=ALU.mult)

        def quantise(c):
            codes[c] = []
            for key in ("sq", "x"):
                words = code_pool.tile(
                    [P, CU * UNIT_WORDS], U32, name=key + "_words", tag=key + "_words", align_bytes=64
                )
                scales = code_pool.tile(
                    [P, CU * UNIT_WORDS], U8, name=key + "_scales", tag=key + "_scales", align_bytes=64
                )
                codes[c].append((words, scales))
            for operand, values in ((1, x_bf16[c]), (0, sq_bf16[c])):
                words, scales = codes[c][operand]
                nc.vector.quantize_mx(out=words[:].bitcast(FP8X4), scales=scales[:], in_=values[:])

        def multiply(c, t):
            if t == 0:
                results[c] = result_psum.tile([P, CU * COMPS], F32, name="result_bank", tag="result_bank")
            last = 2 * PASSES - 1
            for n in range(last + 1):
                operand, g = divmod(n, PASSES)
                words, scales = codes[c][operand]
                unit_cols = slice(t * UNIT_WORDS + g * P, t * UNIT_WORDS + (g + 1) * P)
                w_cols = slice(n * COMPS, (n + 1) * COMPS)
                nc.tensor.matmul_mx(
                    out=results[c][:, t * COMPS : (t + 1) * COMPS],
                    lhsT=words[:, unit_cols].bitcast(FP8X4),
                    lhsT_scale=scales[:, unit_cols],
                    rhs=w_words[:, w_cols].bitcast(FP8X4),
                    rhs_scale=w_scales[:, w_cols],
                    start=(n == 0),
                    stop=(n == last),
                )

        def add_and_store(c):
            finished = out_pool.tile([P, CU * COMPS], F32, name="finished", tag="finished")
            nc.vector.tensor_tensor(out=finished[:], in0=results[c][:], in1=constant_rows[:], op=ALU.add)
            rows = out[c * CU * P : (c + 1) * CU * P, :]
            nc.sync.dma_start(out=rows.rearrange("(p t) k -> p (t k)", t=CU), in_=finished[:])


        def as_in_dram(tile_ap, g):
            return tile_ap[:, g * K_PASS : (g + 1) * K_PASS].rearrange("k (w e) -> k e w", e=2)

        def in_planes(tile_ap, g):
            return tile_ap[:, g * K_PASS : (g + 1) * K_PASS].rearrange("k (e w) -> k e w", e=2)

        def invert(g):
            nc.vector.reciprocal(out=in_planes(inv_var, g), in_=as_in_dram(var_sb, g))

        def times_mean(g):
            nc.vector.tensor_tensor(
                out=in_planes(mean_inv_var, g), in0=as_in_dram(mean_sb, g), in1=in_planes(inv_var, g), op=ALU.mult
            )
            nc.vector.scalar_tensor_tensor(
                out=in_planes(mean2_inv_var, g),
                in0=as_in_dram(mean_sb, g),
                scalar=1.0,
                in1=in_planes(mean_inv_var, g),
                op0=ALU.mult,
                op1=ALU.mult,
                accum_out=c_part[g][:],
            )

        def transpose_weights(g):
            for operand, values in enumerate((inv_var, mean_inv_var)):
                bank = result_psum.tile([P, PACK * COMPS], F32, name="result_bank", tag="result_bank")
                for h in range(2):
                    for e in range(2):
                        src = g * K_PASS + e * (K_PASS // 2) + h * P
                        dst = (2 * h + e) * P
                        nc.tensor.transpose(bank[:, dst : dst + P], values[:, src : src + P], ident[:])
                w_banks[(g, operand)] = bank

        def empty_weights(g):
            for operand in range(2):
                n = PASSES * operand + g
                nc.scalar.activation(
                    out=w_bf16[:, n * K_PASS : (n + 1) * K_PASS].rearrange("p (k t) -> p k t", t=PACK),
                    in_=w_banks[(g, operand)][:].rearrange("p (t k) -> p k t", t=PACK),
                    func=ACT.Copy,
                    scale=(-0.5, 1.0)[operand],
                )

        def first_weights_out():
            empty_weights(0)
            transpose_weights(1)

        def second_weights_out():
            empty_weights(1)
            nc.vector.tensor_tensor(out=sums[:], in0=c_part[0][:], in1=c_part[1][:], op=ALU.add)
            nc.vector.tensor_tensor(out=sums[:], in0=sums[:], in1=log_sum[:], op=ALU.add)
            nc.vector.tensor_scalar(
                out=constant[:],
                in0=sums[:],
                scalar1=-0.5,
                scalar2=-0.5 * D * math.log(2.0 * math.pi),
                op0=ALU.mult,
                op1=ALU.add,
            )
            nc.scalar.activation(
                out=constant_wide[:], in_=ident[:], func=ACT.Identity, scale=0.0, bias=constant[:, 0:1]
            )
            w_banks["constant"] = result_psum.tile([P, CU * COMPS], F32, name="result_bank", tag="result_bank")
            for t in range(CU):
                nc.tensor.transpose(w_banks["constant"][:, t * P : (t + 1) * P], constant_wide[:], ident[:])

        def constant_out():
            nc.scalar.copy(out=constant_rows[:], in_=w_banks["constant"][:])

        def slot(s, extra=()):
            if 1 <= s <= CHUNKS:
                quantise(s - 1)
            if 3 <= s:
                add_and_store(s - 3)
            if s == 2:
                nc.vector.quantize_mx(out=w_words[:].bitcast(FP8X4), scales=w_scales[:], in_=w_bf16[:])
            for t in range(CU):
                if t % 2 == 0 and 2 <= s <= CHUNKS + 1:
                    multiply(s - 2, t)
                    multiply(s - 2, t + 1)
                if s < CHUNKS:
                    empty_unit(s * CU + t)
                    if s * CU + t + UNIT_BANKS < UNITS:
                        transpose_unit(s * CU + t + UNIT_BANKS)
                    for when, step in extra:
                        if when == t:
                            step()
            if s < CHUNKS:
                square_rest(s)

        make_identity(nc, ident[:])
        nc.scalar.dma_start(out=var_sb[:], in_=var)
        load(0, 2)
        nc.scalar.dma_start(out=mean_sb[:], in_=mean)
        for c in range(1, X_BUFS):
            load(c, 1)
        nc.scalar.activation(out=logs[:], in_=var_sb[:], func=ACT.Ln, accum_out=log_sum[:])
        for g in range(PASSES):
            invert(g)
        for g in range(PASSES):
            times_mean(g)
        for u in range(UNIT_BANKS):
            transpose_unit(u)
        slot(0, extra=((1, lambda: transpose_weights(0)),))
        slot(1, extra=((2, first_weights_out), (3, second_weights_out)))
        slot(2, extra=((0, constant_out),))
        for s in range(3, CHUNKS + 3):
            slot(s)
